import numpy as np
import ml_dtypes


def mxq(x, axis, fmt="e4m3"):
    dtype, down = {"e4m3": (ml_dtypes.float8_e4m3fn, 7), "e5m2": (ml_dtypes.float8_e5m2, 14)}[fmt]
    v = np.moveaxis(np.asarray(x, np.float32).astype(ml_dtypes.bfloat16).astype(np.float64), axis, -1)
    blocks = v.reshape(v.shape[:-1] + (-1, 32))
    amax = np.abs(blocks).max(-1, keepdims=True)
    byte = np.maximum(np.where(amax > 0, np.frexp(amax)[1] - 1 + 127, 0) - down, 1)
    scale = np.exp2(byte - 127.0)
    codes = (blocks / scale).astype(np.float32).astype(dtype).astype(np.float64)
    return np.moveaxis((codes * scale).reshape(v.shape), -1, axis)


WIDE = False


def mx_kscale(k, group=512):
    if not WIDE:
        return np.ones(k)
    levels = np.array([10, -10, 5, -5, 0])
    if group != 512:
        return np.exp2(np.random.permutation(np.resize(levels, k // group))).repeat(group)
    if k % 512:
        return np.exp2(np.random.permutation(np.resize(levels, k // 32))).repeat(32)
    a = np.empty((k // 512, 16))
    for p in range(k // 512):
        a[p, :8] = np.random.permutation(np.resize(levels, 8))
        for g in range(8):
            far = levels[np.abs(levels - a[p, g]) >= 10]
            a[p, g + 8] = far[np.random.randint(len(far))]
    return np.exp2(a.ravel()).repeat(32)


BF16 = ml_dtypes.bfloat16


def bf(x):
    return np.asarray(x, np.float32).astype(BF16)


def f64(x):
    return np.asarray(x).astype(np.float64)


B, S, T, E, D, H = 1, 512, 512, 2048, 2048, 16
DK = D // H


def rope_tables(n):
    m = np.arange(n, dtype=np.float64)[:, None]
    i = np.repeat(np.arange(DK // 2, dtype=np.float64), 2)[None, :]
    ang = m * np.exp(-(2.0 * np.log(1e4) / DK) * i)
    return np.cos(ang), np.sin(ang)


def rotate_pairs(x):
    return np.stack([-x[..., 1::2], x[..., 0::2]], axis=-1).reshape(x.shape)


def setup_inputs():
    s = mx_kscale(S, group=128)
    u = np.repeat(mx_kscale(D)[0::2], 2)
    x0 = bf(np.random.standard_normal((B, S, E)))
    w0 = bf(np.random.standard_normal((E, D)) * 1.1 / np.sqrt(E))
    b = bf(np.random.standard_normal(D) * 0.4)
    g = np.random.standard_normal((B, H, S, DK)) * np.exp2(np.random.randint(-6, 1, (B, 1, S, 1))) * 4.0
    g = bf(g / s[None, None, :, None] * u.reshape(1, H, 1, DK))
    return {"x": bf(f64(x0) * s[None, :, None]), "w": bf(f64(w0) / u[None, :]), "b": b, "grad_out": g}


def reference(x, w, b, grad_out):
    r1, r2 = rope_tables(S)
    g = f64(grad_out)
    dp = g * r1 - rotate_pairs(g) * r2
    dz = dp.transpose(0, 2, 1, 3).reshape(B * S, D)
    xf = f64(x).reshape(B * S, E)
    dx = mxq(dz, 1, "e5m2") @ mxq(f64(w), 1, "e4m3").T
    dw = mxq(xf, 0, "e4m3").T @ mxq(dz, 0, "e5m2")
    return dx.reshape(B, S, E), dw

import math
from contextlib import ExitStack

import concourse.mybir as mybir
from concourse.masks import make_identity

S, E, D, H = 512, 2048, 2048, 16
DK = D // H
P = 128
J = 4
C = 4
Q = 4

F32 = mybir.dt.float32
BF16 = mybir.dt.bfloat16
I32 = mybir.dt.int32
U32 = mybir.dt.uint32
U8 = mybir.dt.uint8
E4M3 = mybir.dt.float8_e4m3fn_x4
E5M2 = mybir.dt.float8_e5m2_x4
ADD = mybir.AluOpType.add
SUB = mybir.AluOpType.subtract
MULT = mybir.AluOpType.mult
SIN = mybir.ActivationFunctionType.Sin

FLOPS = 2 * 2 * S * E * D
MANUAL = True
XPE = True
RAW = 6
WG = 6


PLAN = [
    ('V', 'tab'),
    ('Y', 'ldg00'),
    ('Y', 'ldg01'),
    ('Y', 'ldg1'),
    ('Y', 'ldx0'),
    ('V', 'mul', 0, 0),
    ('V', 'mul', 0, 1),
    ('Y', 'ldw0'),
    ('S', 'xint', 0),
    ('V', 'add', 0, 0),
    ('Y', 'ldw1'),
    ('V', 'add', 0, 1),
    ('V', 'mul', 1, 0),
    ('S', 'xint', 1),
    ('T', 'dtr', 0),
    ('Y', 'ldx1'),
    ('T', 'wtr', 0, 0),
    ('V', 'inter', 0),
    ('S', 'dev', 0, 0),
    ('Y', 'ldw2'),
    ('S', 'dev', 0, 1),
    ('T', 'wtr', 0, 1),
    ('V', 'add', 1, 0),
    ('S', 'wev', 0, 0, 0),
    ('T', 'wtr', 0, 2),
    ('S', 'wev', 0, 0, 1),
    ('V', 'qf', 0),
    ('S', 'wev', 0, 1, 0),
    ('Y', 'ldw3'),
    ('V', 'qx', 0),
    ('T', 'wtr', 0, 3),
    ('S', 'wev', 0, 1, 1),
    ('V', 'mul', 1, 1),
    ('S', 'wev', 0, 2, 0),
    ('S', 'wev', 0, 2, 1),
    ('S', 'wev', 0, 3, 0),
    ('Y', 'ldg2'),
    ('S', 'wev', 0, 3, 1),
    ('V', 'qx', 1),
    ('S', 'xint', 2),
    ('V', 'add', 1, 1),
    ('Y', 'ldw4'),
    ('T', 'wtr', 1, 0),
    ('V', 'qt', 0),
    ('T', 'dtr', 1),
    ('V', 'inter', 1),
    ('S', 'wev', 1, 0, 0),
    ('Y', 'ldw5'),
    ('S', 'wev', 1, 0, 1),
    ('T', 'wtr', 1, 1),
    ('V', 'dev', 1, 0),
    ('S', 'dev', 1, 1),
    ('V', 'qt', 1),
    ('S', 'xint', 3),
    ('T', 'wtr', 1, 2),
    ('V', 'qf', 1),
    ('Y', 'ldg3'),
    ('V', 'qx', 2),
    ('T', 'o1', 0, 0),
    ('V', 'mul', 2, 0),
    ('T', 'o1', 1, 0),
    ('Y', 'ldw6'),
    ('S', 'wev', 1, 1, 0),
    ('S', 'wev', 1, 1, 1),
    ('S', 'e1', 0, 0, 0),
    ('T', 'o1', 2, 0),
    ('V', 'qx', 3),
    ('S', 'e1', 0, 0, 1),
    ('V', 'add', 2, 0),
    ('Y', 'ldw7'),
    ('S', 'e1', 1, 0, 0),
    ('T', 'o1', 3, 0),
    ('S', 'e1', 1, 0, 1),
    ('V', 'qw', 0, 0),
    ('S', 'e1', 2, 0, 0),
    ('T', 'wtr', 1, 3),
    ('V', 'qw', 0, 1),
    ('S', 'wev', 1, 2, 0),
    ('V', 'mul', 2, 1),
    ('S', 'wev', 1, 2, 1),
    ('Y', 's1', 0, 0),
    ('T', 'o1', 4, 0),
    ('S', 'wev', 1, 3, 0),
    ('S', 'wev', 1, 3, 1),
    ('Y', 's1', 1, 0),
    ('T', 'wtr', 2, 0),
    ('S', 'e1', 2, 0, 1),
    ('V', 'qw', 0, 2),
    ('S', 'e1', 3, 0, 0),
    ('T', 'o1', 5, 0),
    ('V', 'add', 2, 1),
    ('S', 'e1', 3, 0, 1),
    ('Y', 's1', 2, 0),
    ('S', 'wev', 2, 0, 0),
    ('T', 'o1', 6, 0),
    ('V', 'qw', 0, 3),
    ('S', 'wev', 2, 0, 1),
    ('Y', 's1', 3, 0),
    ('V', 'inter', 2),
    ('S', 'e1', 4, 0, 0),
    ('T', 'dtr', 2),
    ('S', 'e1', 4, 0, 1),
    ('S', 'e1', 5, 0, 0),
    ('V', 'mul', 3, 0),
    ('T', 'wtr', 2, 1),
    ('S', 'dev', 2, 0),
    ('Y', 's1', 4, 0),
    ('S', 'dev', 2, 1),
    ('T', 'o1', 7, 0),
    ('S', 'e1', 5, 0, 1),
    ('S', 'e1', 6, 0, 0),
    ('V', 'qf', 2),
    ('T', 'o1', 8, 0),
    ('S', 'e1', 6, 0, 1),
    ('V', 'add', 3, 0),
    ('Y', 's1', 5, 0),
    ('S', 'wev', 2, 1, 0),
    ('T', 'wtr', 2, 2),
    ('S', 'wev', 2, 1, 1),
    ('V', 'qt', 2),
    ('Y', 's1', 6, 0),
    ('S', 'e1', 7, 0, 0),
    ('V', 'qw', 1, 0),
    ('T', 'o1', 9, 0),
    ('S', 'e1', 7, 0, 1),
    ('V', 'e1', 8, 0, 0),
    ('S', 'e1', 8, 0, 1),
    ('V', 'wev', 2, 2, 0),
    ('T', 'o1', 10, 0),
    ('S', 'wev', 2, 2, 1),
    ('V', 'e1', 9, 0, 0),
    ('T', 'wtr', 2, 3),
    ('Y', 's1', 7, 0),
    ('S', 'e1', 9, 0, 1),
    ('V', 'qw', 1, 1),
    ('S', 'e1', 10, 0, 0),
    ('V', 'mul', 3, 1),
    ('T', 'o1', 11, 0),
    ('Y', 's1', 8, 0),
    ('S', 'e1', 10, 0, 1),
    ('T', 'o1', 12, 0),
    ('S', 'wev', 2, 3, 0),
    ('T', 'wtr', 3, 0),
    ('Y', 's1', 9, 0),
    ('S', 'wev', 2, 3, 1),
    ('S', 'e1', 11, 0, 0),
    ('V', 'e1', 11, 0, 1),
    ('Y', 's1', 10, 0),
    ('T', 'o1', 13, 0),
    ('S', 'e1', 12, 0, 0),
    ('V', 'add', 3, 1),
    ('S', 'e1', 12, 0, 1),
    ('T', 'o1', 14, 0),
    ('Y', 's1', 11, 0),
    ('S', 'e1', 13, 0, 0),
    ('V', 'qw', 1, 2),
    ('T', 'wtr', 3, 1),
    ('S', 'e1', 13, 0, 1),
    ('V', 'inter', 3),
    ('S', 'wev', 3, 0, 0),
    ('Y', 's1', 12, 0),
    ('T', 'dtr', 3),
    ('S', 'wev', 3, 0, 1),
    ('V', 'e1', 14, 0, 0),
    ('S', 'e1', 14, 0, 1),
    ('Y', 's1', 13, 0),
    ('T', 'o1', 15, 0),
    ('V', 'qt', 3),
    ('S', 'dev', 3, 0),
    ('T', 'wtr', 3, 2),
    ('V', 'dev', 3, 1),
    ('S', 'e1', 15, 0, 0),
    ('Y', 's1', 14, 0),
    ('V', 'qw', 1, 3),
    ('S', 'e1', 15, 0, 1),
    ('T', 'o1', 0, 1),
    ('V', 'qf', 3),
    ('S', 'wev', 3, 1, 0),
    ('V', 'wev', 3, 1, 1),
    ('T', 'o1', 1, 1),
    ('S', 'e1', 0, 1, 0),
    ('Y', 's1', 15, 0),
    ('V', 'e1', 0, 1, 1),
    ('T', 'o0', 0, 0),
    ('S', 'e1', 1, 1, 0),
    ('V', 'e1', 1, 1, 1),
    ('V', 'qw', 2, 0),
    ('T', 'o1', 2, 1),
    ('S', 'e0', 0, 0),
    ('Y', 's1', 0, 1),
    ('T', 'o1', 3, 1),
    ('V', 'qw', 2, 1),
    ('S', 'e1', 2, 1, 0),
    ('T', 'o1', 4, 1),
    ('V', 'e1', 2, 1, 1),
    ('S', 'e1', 3, 1, 0),
    ('Y', 's1', 1, 1),
    ('T', 'o0', 1, 0),
    ('V', 'e1', 3, 1, 1),
    ('S', 'e1', 4, 1, 0),
    ('V', 'e1', 4, 1, 1),
    ('S', 'wev', 3, 2, 0),
    ('Y', 's1', 2, 1),
    ('T', 'o1', 5, 1),
    ('V', 'wev', 3, 2, 1),
    ('S', 'e0', 1, 0),
    ('T', 'o1', 6, 1),
    ('V', 'qw', 2, 2),
    ('S', 'e1', 5, 1, 0),
    ('Y', 's1', 3, 1),
    ('T', 'o1', 7, 1),
    ('V', 'e1', 5, 1, 1),
    ('S', 'e1', 6, 1, 0),
    ('T', 'o1', 8, 1),
    ('V', 'e1', 6, 1, 1),
    ('Y', 's1', 4, 1),
    ('T', 'o0', 0, 1),
    ('V', 'qw', 2, 3),
    ('S', 'e1', 7, 1, 0),
    ('V', 'e1', 7, 1, 1),
    ('T', 'o1', 9, 1),
    ('Y', 's0', 0, 0),
    ('V', 'qw', 3, 0),
    ('S', 'e1', 8, 1, 0),
    ('T', 'o0', 1, 1),
    ('V', 'e1', 8, 1, 1),
    ('Y', 's1', 5, 1),
    ('V', 'qw', 3, 1),
    ('T', 'o1', 10, 1),
    ('S', 'e1', 9, 1, 0),
    ('V', 'e1', 9, 1, 1),
    ('T', 'o0', 0, 2),
    ('Y', 's1', 6, 1),
    ('V', 'qw', 3, 2),
    ('S', 'e1', 10, 1, 0),
    ('V', 'e1', 10, 1, 1),
    ('T', 'o0', 1, 2),
    ('S', 'e0', 1, 1),
    ('Y', 's1', 7, 1),
    ('V', 'e0', 0, 1),
    ('T', 'o1', 11, 1),
    ('Y', 's1', 8, 1),
    ('T', 'o0', 0, 3),
    ('S', 'e1', 11, 1, 1),
    ('V', 'e1', 11, 1, 0),
    ('S', 'e0', 1, 2),
    ('Y', 's1', 9, 1),
    ('T', 'o1', 12, 1),
    ('V', 'e0', 0, 2),
    ('T', 'o0', 1, 3),
    ('S', 'e1', 12, 1, 1),
    ('Y', 's1', 10, 1),
    ('V', 'e1', 12, 1, 0),
    ('T', 'wtr', 3, 3),
    ('S', 'e0', 1, 3),
    ('Y', 's0', 0, 1),
    ('V', 'e0', 0, 3),
    ('T', 'o0', 2, 0),
    ('S', 'wev', 3, 3, 0),
    ('V', 'wev', 3, 3, 1),
    ('Y', 's1', 11, 1),
    ('V', 'qw', 3, 3),
    ('T', 'o1', 13, 1),
    ('S', 'e0', 2, 0),
    ('Y', 's0', 0, 2),
    ('T', 'o1', 14, 1),
    ('S', 'e1', 13, 1, 1),
    ('V', 'e1', 13, 1, 0),
    ('T', 'o0', 3, 0),
    ('S', 'e1', 14, 1, 1),
    ('Y', 's1', 12, 1),
    ('V', 'e1', 14, 1, 0),
    ('T', 'o0', 2, 1),
    ('S', 'e0', 3, 0),
    ('Y', 's0', 0, 3),
    ('T', 'o0', 3, 1),
    ('V', 'e0', 2, 1),
    ('Y', 's1', 13, 1),
    ('T', 'o1', 15, 1),
    ('V', 'e0', 3, 1),
    ('T', 'o0', 2, 2),
    ('Y', 's1', 14, 1),
    ('V', 'e1', 15, 1, 0),
    ('S', 'e1', 15, 1, 1),
    ('T', 'o0', 3, 2),
    ('V', 'e0', 2, 2),
    ('Y', 's0', 1, 0),
    ('T', 'o0', 2, 3),
    ('V', 'e0', 3, 2),
    ('Y', 's0', 1, 1),
    ('T', 'o0', 3, 3),
    ('V', 'e0', 2, 3),
    ('Y', 's1', 15, 1),
    ('V', 'e0', 3, 3),
    ('Y', 's0', 1, 2),
    ('Y', 's0', 1, 3),
]


def tile_multiheadedattention_pa_v_kernel(tc, x, w, b, grad_out, out_0, out_1):
    nc = tc.nc
    with ExitStack() as ctx:
        keep = ctx.enter_context(tc.tile_pool(name="keep", bufs=1))
        pool = ctx.enter_context(tc.tile_pool(name="pool", bufs=2))
        psum = ctx.enter_context(tc.psum_pool(name="psum", bufs=8))
        if MANUAL:
            ctx.enter_context(tc.manual_schedule())

        def load_g(c, h0, h1, tile):
            src = grad_out[0, C * c + h0 : C * c + h1].rearrange("h (p j) d -> p h (j d)", j=J)
            nc.sync.dma_start(out=tile[:, h0:h1, :], in_=src)

        g_t = {}

        def alloc_g(c):
            g_tile = pool.tile([P, 4, J * DK], BF16, tag="g", bufs=3, align_bytes=64, name="g_tile")
            g_t[c] = g_tile

        x_t = {}

        def load_x(u):
            x_tile = pool.tile([P, J, 1024], BF16, tag="raw", bufs=RAW, align_bytes=64, name="x_tile")
            nc.sync.dma_start(out=x_tile[:], in_=x[0, :, 1024 * u : 1024 * (u + 1)].rearrange("(p j) e -> p j e", j=J))
            x_t[u] = x_tile

        w_t = {}

        def load_w(k):
            w_tile = pool.tile([P, 2, D], BF16, tag="raw", bufs=RAW, align_bytes=64, name="w_tile")
            nc.sync.dma_start(out=w_tile[:], in_=w[256 * k : 256 * (k + 1), :].rearrange("(r e) d -> r e d", e=2))
            w_t[k] = w_tile


        pos = keep.tile([P, J, 2], I32, name="pos")
        ident = keep.tile([P, P], F32, align_bytes=64, name="ident")
        cos_t = keep.tile([P, J, DK // 2, 2], F32, align_bytes=64, name="cos_t")
        sin_t = keep.tile([P, J, DK // 2, 2], F32, align_bytes=64, name="sin_t")

        def stage(shape, dtype, name):
            st = pool.tile(shape, dtype, tag="st", bufs=6, align_bytes=64, name=name)
            return st

        def tables():
            nc.gpsimd.iota(pos[:, :, 0], pattern=[[1, J]], base=0, channel_multiplier=J)
            nc.gpsimd.iota(pos[:, :, 1], pattern=[[-1, J]], base=0, channel_multiplier=-J)
            make_identity(nc, ident[:])
            warm = keep.tile([P, 2], F32, name="warm")
            nc.vector.memset(warm[:, 0:1], 0.0)
            nc.scalar.activation(out=warm[:, 1:2], in_=warm[:, 0:1], func=SIN)
            turns = stage([P, J, DK // 2, 2], F32, "turns")
            for i in range(8):
                t_i = math.exp(-(2.0 * math.log(1e4) / DK) * i) / (2.0 * math.pi)
                nc.vector.tensor_scalar(out=turns[:, :, i, :], in0=pos[:], scalar1=t_i, scalar2=None, op0=MULT)
            for k in range(1, 8):
                ratio = math.exp(-(2.0 * math.log(1e4) / DK) * 8 * k)
                nc.vector.tensor_scalar(
                    out=turns[:, :, 8 * k : 8 * k + 8, :], in0=turns[:, :, 0:8, :], scalar1=ratio, scalar2=None, op0=MULT
                )
            flat = "p j i e -> p (j i e)"
            half = [P, J, DK // 2]
            whole_c = stage(half, I32, "whole_c")
            whole_s = stage([P, J * DK], I32, "whole_s")
            frac_c = stage(half, F32, "frac_c")
            frac_s = stage([P, J * DK], F32, "frac_s")
            tf = turns[:].rearrange(flat)
            nc.vector.tensor_scalar(out=whole_c[:], in0=turns[:, :, :, 0], scalar1=0.25, scalar2=None, op0=ADD)
            nc.vector.tensor_copy(out=whole_s[:], in_=tf)
            nc.vector.scalar_tensor_tensor(out=frac_c[:], in0=turns[:, :, :, 0], scalar=0.25, in1=whole_c[:], op0=ADD, op1=SUB)
            nc.vector.tensor_tensor(out=frac_s[:], in0=tf, in1=whole_s[:], op=SUB)
            both = frac_c[:].rearrange("p j i -> p (j i)").unsqueeze(2).to_broadcast([P, J * DK // 2, 2])
            nc.scalar.activation(out=cos_t[:].rearrange("p j i e -> p (j i) e"), in_=both, func=SIN, scale=2.0 * math.pi)
            nc.scalar.activation(out=sin_t[:].rearrange(flat), in_=frac_s[:], func=SIN, scale=2.0 * math.pi)

        xc = keep.tile([P, E], U32, align_bytes=64, name="xc")
        xs = keep.tile([P, E], U8, align_bytes=64, name="xs")
        dt_c = keep.tile([P, C, 512], U32, align_bytes=64, name="dt_c")
        dt_s = keep.tile([P, C, 512], U8, align_bytes=64, name="dt_s")
        df_c = keep.tile([P, C, S], U32, align_bytes=64, name="df_c")
        df_s = keep.tile([P, C, S], U8, align_bytes=64, name="df_s")
        wc = keep.tile([P, Q, C, 512], U32, align_bytes=64, name="wc")
        ws = keep.tile([P, Q, C, 512], U8, align_bytes=64, name="ws")

        def copy(engine, out, in_):
            if engine == "S":
                nc.scalar.copy(out=out, in_=in_)
            else:
                nc.vector.tensor_copy(out=out, in_=in_)

        prod = {}
        dzb = {}

        def dz_mul(c, hp):
            a_tile = pool.tile([P, 2, J * DK], F32, tag="pa", bufs=2, align_bytes=64, name="a_tile")
            b_tile = pool.tile([P, 2, J * DK], F32, tag="pb", bufs=2, align_bytes=64, name="b_tile")
            g = g_t[c][:, 2 * hp : 2 * hp + 2, :]
            shape = [P, 2, J * DK // 2, 2]
            ct = cos_t[:].rearrange("p j i e -> p (j i) e").unsqueeze(1).to_broadcast(shape)
            st = sin_t[:].rearrange("p j i e -> p (j i) e").unsqueeze(1).to_broadcast(shape)
            g4 = g.rearrange("p h (x e) -> p h x e", e=2)
            nc.vector.tensor_tensor(out=a_tile[:].rearrange("p h (x e) -> p h x e", e=2), in0=g4, in1=ct, op=MULT)
            nc.vector.tensor_tensor(out=b_tile[:].rearrange("p h (x e) -> p h x e", e=2), in0=g4[:, :, :, ::-1], in1=st, op=MULT)
            prod[c, hp] = (a_tile, b_tile)

        def dz_add(c, hp):
            if hp == 0:
                dz_tile = pool.tile([P, J, 512], BF16, tag="dz", bufs=2, align_bytes=64, name="dz_tile")
                dzb[c] = dz_tile
            a_tile, b_tile = prod[c, hp]
            out = dzb[c][:, :, 256 * hp : 256 * (hp + 1)].rearrange("p j (h d) -> p h j d", d=DK)
            nc.vector.tensor_tensor(
                out=out,
                in0=a_tile[:].rearrange("p h (j d) -> p h j d", d=DK),
                in1=b_tile[:].rearrange("p h (j d) -> p h j d", d=DK),
                op=ADD,
            )

        dzi = {}

        def dz_inter(c):
            di_tile = pool.tile([P, 512, J], BF16, tag="dzi", bufs=2, align_bytes=64, name="di_tile")
            nc.vector.tensor_copy(out=di_tile[:], in_=dzb[c][:].rearrange("p j f -> p f j"))
            dzi[c] = di_tile

        def dz_qtok(c):
            nc.vector.quantize_mx(
                out=dt_c[:, c, :].bitcast(E5M2), scales=dt_s[:, c, :], in_=dzi[c][:].rearrange("p f j -> p (f j)")
            )

        banks = {}

        def dz_tr(c):
            words = dzb[c][:].rearrange("p j f -> p (j f)").bitcast(F32)
            for k in range(2):
                bank = psum.tile([P, 2, 2, P], F32, tag="bank", bufs=8, name="bank")
                for jj in range(2):
                    for u in range(2):
                        first = 256 * (2 * k + jj) + u
                        last = 256 * (2 * k + jj + 1)
                        nc.tensor.transpose(bank[:, jj, u, :], words[:, first:last:2], ident[:])
                banks["d", c, k] = bank

        dzf = {}

        def dz_ev(c, k, engine):
            if c not in dzf:
                df_tile = pool.tile([P, J, P, 4], BF16, tag="dzf", bufs=2, align_bytes=64, name="df_tile")
                dzf[c] = df_tile
            out = dzf[c][:, 2 * k : 2 * k + 2].rearrange("p j r t -> p (j r t)").bitcast(F32)
            out = out.rearrange("p (j r u) -> p j r u", j=2, u=2)
            copy(engine, out, banks["d", c, k][:].rearrange("p j u r -> p j r u"))

        def dz_qfeat(c):
            nc.vector.quantize_mx(
                out=df_c[:, c, :].bitcast(E5M2), scales=df_s[:, c, :], in_=dzf[c][:].rearrange("p j r t -> p (j r t)")
            )

        xi = {}

        def x_inter(q, engine):
            xi_tile = pool.tile([P, 512, J], BF16, tag="xi", bufs=2, align_bytes=64, name="xi_tile")
            src = x_t[q // 2][:, :, 512 * (q % 2) : 512 * (q % 2 + 1)].rearrange("p j e -> p e j")
            copy(engine, xi_tile[:], src)
            xi[q] = xi_tile

        ident_b = keep.tile([P, P], BF16, align_bytes=64, name="ident_b")
        if XPE:
            make_identity(nc, ident_b[:])

        def x_pe(q):
            for k in range(2):
                bank = psum.tile([P, 256, J], BF16, tag="bank", bufs=8, name="bank")
                for j in range(J):
                    first = 512 * (q % 2) + 256 * k
                    nc.tensor.matmul(out=bank[:, :, j], lhsT=ident_b[:], rhs=x_t[q // 2][:, j, first : first + 256], start=True, stop=True)
                banks["x", q, k] = bank

        def x_ev(q, k, engine):
            if q not in xi:
                xi_tile = pool.tile([P, 512, J], BF16, tag="xi", bufs=2, align_bytes=64, name="xi_tile")
                xi[q] = xi_tile
            copy(engine, xi[q][:, 256 * k : 256 * (k + 1), :], banks["x", q, k][:])

        def x_q(q):
            cols = slice(512 * q, 512 * (q + 1))
            nc.vector.quantize_mx(out=xc[:, cols].bitcast(E4M3), scales=xs[:, cols], in_=xi[q][:].rearrange("p e j -> p (e j)"))

        def w_tr(q, g):
            for k in range(2):
                words = w_t[2 * q + k][:].rearrange("p e d -> p (e d)").bitcast(F32)
                bank = psum.tile([P, 2, 2, P], F32, tag="bank", bufs=8, name="bank")
                for e in range(2):
                    for u in range(2):
                        first = 1024 * e + 256 * g + u
                        last = 1024 * e + 256 * (g + 1)
                        nc.tensor.transpose(bank[:, e, u, :], words[:, first:last:2], ident[:])
                banks["w", q, g, k] = bank

        wg = {}

        def w_ev(q, g, k, engine):
            if (q, g) not in wg:
                wg_tile = pool.tile([P, 2, 2, P, 4], BF16, tag="wg", bufs=WG, align_bytes=64, name="wg_tile")
                wg[q, g] = wg_tile
            out = wg[q, g][:, k].rearrange("p e r t -> p (e r t)").bitcast(F32)
            out = out.rearrange("p (e r u) -> p e r u", e=2, u=2)
            copy(engine, out, banks["w", q, g, k][:].rearrange("p e u r -> p e r u"))

        def w_q(q, g):
            nc.vector.quantize_mx(
                out=wc[:, q, g, :].bitcast(E4M3), scales=ws[:, q, g, :], in_=wg[q, g][:].rearrange("p k e r t -> p (k e r t)")
            )

        outs = {}

        def o1_mm(et, c):
            bank = psum.tile([P, 512], F32, tag="bank", bufs=8, name="bank")
            rows = slice(P * et, P * (et + 1))
            nc.tensor.matmul_mx(
                out=bank[:],
                lhsT=xc[:, rows].bitcast(E4M3),
                lhsT_scale=xs[:, rows],
                rhs=dt_c[:, c, :].bitcast(E5M2),
                rhs_scale=dt_s[:, c, :],
                start=True,
                stop=True,
            )
            banks["1", et, c] = bank

        def o1_ev(et, c, engine):
            if (et, c // 2) not in outs:
                outs[et, c // 2] = stage([P, 1024], F32, "o1_tile")
            copy(engine, outs[et, c // 2][:, 512 * (c % 2) : 512 * (c % 2 + 1)], banks["1", et, c][:])

        def o1_st(et, half):
            nc.sync.dma_start(
                out=out_1[P * et : P * (et + 1), 1024 * half : 1024 * (half + 1)], in_=outs[et, half][:]
            )

        def o0_mm(q, j):
            bank = psum.tile([P, 2, 2, P], F32, tag="bank", bufs=8, name="bank")
            cols = slice(P * j, P * (j + 1))
            for g in range(C):
                nc.tensor.matmul_mx(
                    out=bank[:].rearrange("p k e r -> p (k e r)"),
                    lhsT=df_c[:, g, cols].bitcast(E5M2),
                    lhsT_scale=df_s[:, g, cols],
                    rhs=wc[:, q, g, :].bitcast(E4M3),
                    rhs_scale=ws[:, q, g, :],
                    start=(g == 0),
                    stop=(g == C - 1),
                )
            banks["0", q, j] = bank

        def o0_ev(q, j, engine):
            if ("0", q // 2, j) not in outs:
                outs["0", q // 2, j] = stage([P, 1024], F32, "o0_tile")
            out = outs["0", q // 2, j][:, 512 * (q % 2) : 512 * (q % 2 + 1)].rearrange("p (k r e) -> p k r e", k=2, e=2)
            copy(engine, out, banks["0", q, j][:].rearrange("p k e r -> p k r e"))

        def o0_st(q2, j):
            dst = out_0[0].rearrange("(p j) e -> p j e", j=J)[:, j, 1024 * q2 : 1024 * (q2 + 1)]
            nc.sync.dma_start(out=dst, in_=outs["0", q2, j][:])

        FN = {
            "mul": dz_mul, "add": dz_add, "inter": dz_inter, "qt": dz_qtok, "qf": dz_qfeat, "dtr": dz_tr, "dev": dz_ev,
            "xpe": x_pe, "xev": x_ev, "xint": x_inter, "qx": x_q, "wtr": w_tr, "wev": w_ev, "qw": w_q, "o0": o0_mm, "e0": o0_ev,
        }
        def load(n):
            if n[2] == "x":
                load_x(int(n[3]))
            elif n[2] == "w":
                load_w(int(n[3]))
            else:
                c = int(n[3])
                if c not in g_t:
                    alloc_g(c)
                h = [0, 4] if len(n) == 4 else [2 * int(n[4]), 2 * int(n[4]) + 2]
                load_g(c, h[0], h[1], g_t[c])

        for e, k, *a in PLAN:
            if e == "Y":
                if k == "s1":
                    o1_st(*a)
                elif k == "s0":
                    o0_st(*a)
                else:
                    load(k)
            elif k == "tab":
                tables()
            elif k == "o1":
                o1_mm(a[0], 2 * a[1])
                o1_mm(a[0], 2 * a[1] + 1)
            elif k == "e1":
                o1_ev(a[0], 2 * a[1] + a[2], e)
            elif k in ("dev", "xint", "xev", "wev", "e0"):
                FN[k](*a, e)
            else:
                FN[k](*a)
